import numpy as np
import ml_dtypes


def mxq(x, axis, fmt="e4m3"):
    dtype, down = {"e4m3": (ml_dtypes.float8_e4m3fn, 7), "e5m2": (ml_dtypes.float8_e5m2, 14)}[fmt]
    v = np.moveaxis(np.asarray(x, np.float32).astype(ml_dtypes.bfloat16).astype(np.float64), axis, -1)
    blocks = v.reshape(v.shape[:-1] + (-1, 32))
    amax = np.abs(blocks).max(-1, keepdims=True)
    byte = np.maximum(np.where(amax > 0, np.frexp(amax)[1] - 1 + 127, 0) - down, 1)
    scale = np.exp2(byte - 127.0)
    codes = (blocks / scale).astype(np.float32).astype(dtype).astype(np.float64)
    return np.moveaxis((codes * scale).reshape(v.shape), -1, axis)


WIDE = False


def mx_kscale(k):
    if not WIDE:
        return np.ones(k)
    levels = np.array([10, -10, 5, -5, 0])
    a = np.random.permutation(np.resize(levels, k // 512 * 4)).reshape(k // 512, 4)
    idx = np.arange(k)
    return np.exp2(a[idx // 512, idx % 128 // 32])


BF16 = ml_dtypes.bfloat16


def bf(x):
    return np.asarray(x, np.float32).astype(BF16)


def f64(x):
    return np.asarray(x).astype(np.float64)


E2M1 = np.array([0.0, 0.5, 1.0, 1.5, 2.0, 3.0, 4.0, 6.0, -0.0, -0.5, -1.0, -1.5, -2.0, -3.0, -4.0, -6.0])


def pack_weight(w, fmt):
    k, n = w.shape
    w = f64(bf(w)).reshape(k // 32, 32, n)
    amax = np.abs(w).max(1)
    if fmt == "e4m3":
        byte = np.frexp(amax)[1] - 1 + 127 - 7
    else:
        mant, ex = np.frexp(amax / 6.0)
        byte = np.where(mant > 0.5, ex, ex - 1) + 127
    byte = np.clip(np.where(amax > 0, byte, 1), 1, 254)
    scaled = (w * np.exp2(127.0 - byte)[:, None, :]).reshape(k, n).astype(np.float32)
    by_word = np.ascontiguousarray(scaled.reshape(k // 512, 128, 4, n).transpose(0, 1, 3, 2))
    if fmt == "e4m3":
        words = by_word.astype(ml_dtypes.float8_e4m3fn).view(np.uint8)
    else:
        c = by_word.astype(ml_dtypes.float4_e2m1fn).view(np.uint8) & 0xF
        words = c[..., 0::2] | (c[..., 1::2] << 4)
    return np.ascontiguousarray(words), np.ascontiguousarray(byte.astype(np.uint8).reshape(k // 512, 16, n))


def unpack_weight(words, scales, fmt):
    g, p, n, _ = words.shape
    if fmt == "e4m3":
        vals = np.ascontiguousarray(words).view(ml_dtypes.float8_e4m3fn).astype(np.float64)
    else:
        nib = np.empty((g, p, n, 4), np.uint8)
        nib[..., 0::2] = words & 0xF
        nib[..., 1::2] = words >> 4
        vals = E2M1[nib]
    vals = vals * np.repeat(np.exp2(scales.astype(np.float64) - 127.0), 8, axis=1)[..., None]
    return vals.transpose(0, 1, 3, 2).reshape(g * 512, n)


N, IN_DIM, HID, OUT_DIM = 1024, 1024, 512, 256


def setup_inputs():
    t = mx_kscale(HID)
    h1 = np.random.standard_normal((1, HID)) * 0.55 + np.random.standard_normal((N, HID)) * 0.55
    A = bf(np.random.uniform(0.0, 1.0, (N, N)) * 0.5 / np.sqrt(N))
    h1 = bf(h1 * t)
    eps1 = bf(np.random.uniform(0.2, 0.4, (1,)))
    words, scales = pack_weight(np.random.standard_normal((HID, HID)) * 0.4 / np.sqrt(HID) / t[:, None], "e4m3")
    b1_1 = bf(np.random.standard_normal(HID) * 0.2)
    return {"A": A,
            "h1": h1,
            "eps1": eps1,
            "W1_1_words": words,
            "W1_1_scales": scales,
            "b1_1": b1_1}


def reference(A, h1, eps1, W1_1_words, W1_1_scales, b1_1):
    x = f64(h1)
    z = (mxq(f64(A), 1, "e4m3") @ mxq(x, 0, "e4m3")) + (1.0 + f64(eps1)) * x
    return np.maximum((mxq(z, 1, "e4m3") @ unpack_weight(W1_1_words, W1_1_scales, "e4m3")) + f64(b1_1), 0.0)

@@ -1,0 +1,220 @@
+from contextlib import ExitStack
+
+import concourse.mybir as mybir
+from concourse.masks import make_identity
+
+F32 = mybir.dt.float32
+BF16 = mybir.dt.bfloat16
+I32 = mybir.dt.int32
+U32 = mybir.dt.uint32
+U8 = mybir.dt.uint8
+FP8X4 = mybir.dt.float8_e4m3fn_x4
+ADD = mybir.AluOpType.add
+MULT = mybir.AluOpType.mult
+RELU = mybir.ActivationFunctionType.Relu
+
+P = 128
+PACK = 4
+HALF = 2
+NODES = 1024
+FEAT = 512
+PASSES = NODES // (P * PACK)
+PAIR = 2
+CHUNKS = NODES // (P * PAIR)
+TILES = CHUNKS * PAIR
+
+FLOPS = 2 * NODES * NODES * FEAT + 2 * NODES * FEAT * FEAT
+
+
+def tile_gin_pb_kernel(tc, A, h1, eps1, W1_1_words, W1_1_scales, b1_1, out):
+    nc = tc.nc
+    with ExitStack() as ctx:
+        keep = ctx.enter_context(tc.tile_pool(name="keep", bufs=1))
+        a_pool = ctx.enter_context(tc.tile_pool(name="a_pool", bufs=CHUNKS))
+        work = ctx.enter_context(tc.tile_pool(name="work", bufs=4))
+        psum_t = ctx.enter_context(tc.psum_pool(name="psum_t", bufs=4))
+        psum_z = ctx.enter_context(tc.psum_pool(name="psum_z", bufs=2))
+        psum_o = ctx.enter_context(tc.psum_pool(name="psum_o", bufs=2))
+        ctx.enter_context(tc.manual_schedule())
+
+        bias_row = keep.tile([P, FEAT], BF16)
+        nc.vector.memset(bias_row[:], 0.0)
+        w_plane = keep.tile([P, FEAT], U8, align_bytes=64)
+        nc.vector.memset(w_plane[:].bitcast(I32), 0)
+        ones = keep.tile([P, P], BF16)
+        nc.vector.memset(ones[:], 1.0)
+        ident = keep.tile([P, P], F32)
+        make_identity(nc, ident[:])
+
+        nc.sync.dma_start(out=bias_row[0:1, :], in_=b1_1.rearrange("(o n) -> o n", o=1))
+        eps_bc = keep.tile([P, 1], BF16)
+        nc.sync.dma_start(out=eps_bc[:], in_=eps1.partition_broadcast(P))
+
+        h1_raw = keep.tile([P, CHUNKS, PAIR, FEAT], BF16)
+        h1_rows = h1.rearrange("(c p e) f -> p c (e f)", p=P, e=PAIR)
+        for g in range(PASSES):
+            nc.sync.dma_start(
+                out=h1_raw[:, 2 * g : 2 * g + 2].rearrange("p c e f -> p c (e f)"),
+                in_=h1_rows[:, 2 * g : 2 * g + 2, :],
+            )
+
+        a_rows = A.rearrange("(c p e) j -> c p (e j)", p=P, e=PAIR)
+        a_tiles = []
+
+        def load_a(c):
+            a_sb = a_pool.tile([P, PAIR, NODES], BF16)
+            nc.sync.dma_start(out=a_sb[:].rearrange("p e j -> p (e j)"), in_=a_rows[c])
+            a_tiles.append(a_sb)
+
+        load_a(0)
+        load_a(1)
+        w_codes = keep.tile([P, FEAT], U32, align_bytes=64)
+        nc.sync.dma_start(
+            out=w_codes[:].bitcast(I32),
+            in_=W1_1_words[0].rearrange("p n t -> p (n t)").bitcast(I32),
+        )
+        for quad in range(4):
+            nc.sync.dma_start(
+                out=w_plane[32 * quad : 32 * quad + 4, :].bitcast(I32),
+                in_=W1_1_scales[0, 4 * quad : 4 * quad + 4, :].bitcast(I32),
+            )
+        load_a(2)
+        load_a(3)
+
+        bias_ps = psum_o.tile([P, FEAT], F32, tag="o_ps")
+        nc.tensor.matmul(bias_ps[:], lhsT=ones[:], rhs=bias_row[:], start=True, stop=True)
+        bias_sb = keep.tile([P, FEAT], F32)
+        nc.scalar.copy(out=bias_sb[:], in_=bias_ps[:])
+
+        h1_grouped = keep.tile([P, PASSES, PACK, P, PACK], BF16, align_bytes=64)
+        h1_codes = keep.tile([P, PASSES, FEAT], U32, align_bytes=64)
+        h1_plane = keep.tile([P, PASSES, FEAT], U8, align_bytes=64)
+        for g in range(PASSES):
+            nc.vector.tensor_copy(
+                out=h1_grouped[:, g].rearrange("q s m t -> q m s t"),
+                in_=h1_raw[:, 2 * g : 2 * g + 2].rearrange("q c e (m s) -> q m s (c e)", s=PACK),
+            )
+        for g in range(PASSES):
+            nc.vector.quantize_mx(
+                out=h1_codes[:, g, :].bitcast(FP8X4),
+                scales=h1_plane[:, g, :],
+                in_=h1_grouped[:, g].rearrange("q s m t -> q (s m t)"),
+            )
+
+        self_w = keep.tile([P, 1], F32)
+        nc.vector.tensor_scalar_add(self_w[:], eps_bc[:], 1.0)
+
+        h1T = keep.tile([P, CHUNKS, PAIR, P, PACK], BF16)
+
+        a_grouped_of = {}
+        a_codes_of = {}
+        z_ps_of = {}
+        z_grouped_of = {}
+        z_codes_of = {}
+        o_ps_of = {}
+
+        def transpose(n):
+            if n < CHUNKS:
+                hT_ps = psum_t.tile([P, PAIR, HALF, P], F32, tag="t_ps")
+                for e in range(PAIR):
+                    for u in range(HALF):
+                        nc.tensor.transpose(
+                            hT_ps[:, e, u, :],
+                            h1_raw[:, n, e, :].bitcast(F32)[:, u : FEAT // HALF : HALF],
+                            ident[:],
+                        )
+                nc.scalar.copy(
+                    out=h1T[:, n].bitcast(F32), in_=hT_ps[:].rearrange("m e u i -> m e i u")
+                )
+            c, e = divmod(n, PAIR)
+            aT_ps = psum_t.tile([P, PASSES * HALF, P], F32, tag="t_ps")
+            for b in range(PASSES * HALF):
+                nc.tensor.transpose(
+                    aT_ps[:, b, :], a_tiles[c][:, e, :].bitcast(F32)[:, P * b : P * (b + 1)], ident[:]
+                )
+            a_grouped = work.tile([P, PASSES, P, PACK], BF16, align_bytes=64)
+            nc.scalar.copy(
+                out=a_grouped[:].bitcast(F32),
+                in_=aT_ps[:].rearrange("q (g u) i -> q g i u", u=HALF),
+            )
+            a_grouped_of[n] = a_grouped
+
+        def aggregate(n):
+            a_codes = work.tile([P, PASSES, P], U32, align_bytes=64)
+            a_plane = work.tile([P, PASSES, P], U8, align_bytes=64)
+            nc.vector.quantize_mx(
+                out=a_codes[:].rearrange("q g i -> q (g i)").bitcast(FP8X4),
+                scales=a_plane[:].rearrange("q g i -> q (g i)"),
+                in_=a_grouped_of[n][:].rearrange("q g i t -> q (g i t)"),
+            )
+            z_ps = psum_z.tile([P, PACK, P], F32)
+            for s in range(PACK):
+                for g in range(PASSES):
+                    nc.tensor.matmul_mx(
+                        out=z_ps[:, s, :],
+                        lhsT=h1_codes[:, g, P * s : P * (s + 1)].bitcast(FP8X4),
+                        lhsT_scale=h1_plane[:, g, P * s : P * (s + 1)],
+                        rhs=a_codes[:, g, :].bitcast(FP8X4),
+                        rhs_scale=a_plane[:, g, :],
+                        start=(g == 0),
+                        stop=(g == PASSES - 1),
+                    )
+            z_ps_of[n] = z_ps
+
+        def add_self(n):
+            c, e = divmod(n, PAIR)
+            z_grouped = work.tile([P, P, PACK], BF16, align_bytes=64)
+            nc.vector.scalar_tensor_tensor(
+                out=z_grouped[:],
+                in0=h1T[:, c, e],
+                scalar=self_w[:, 0:1],
+                in1=z_ps_of[n][:].rearrange("m s i -> m i s"),
+                op0=MULT,
+                op1=ADD,
+            )
+            z_grouped_of[n] = z_grouped
+
+        def quantise_z(n):
+            z_codes = work.tile([P, P], U32, align_bytes=64)
+            z_plane = work.tile([P, P], U8, align_bytes=64)
+            nc.vector.quantize_mx(
+                out=z_codes[:].bitcast(FP8X4),
+                scales=z_plane[:],
+                in_=z_grouped_of[n][:].rearrange("m i s -> m (i s)"),
+            )
+            z_codes_of[n] = (z_codes, z_plane)
+
+        def project(n):
+            z_codes, z_plane = z_codes_of[n]
+            o_ps = psum_o.tile([P, FEAT], F32)
+            nc.tensor.matmul_mx(
+                out=o_ps[:],
+                lhsT=z_codes[:].bitcast(FP8X4),
+                lhsT_scale=z_plane[:],
+                rhs=w_codes[:].bitcast(FP8X4),
+                rhs_scale=w_plane[:],
+                start=True,
+                stop=True,
+            )
+            o_ps_of[n] = o_ps
+
+        out_tiles = out.rearrange("(c p e) n -> c e p n", p=P, e=PAIR)
+
+        def finish(n):
+            c, e = divmod(n, PAIR)
+            o_sb = work.tile([P, FEAT], F32)
+            nc.vector.tensor_tensor(out=o_sb[:], in0=o_ps_of[n][:], in1=bias_sb[:], op=ADD)
+            nc.scalar.activation(out=o_sb[:], in_=o_sb[:], func=RELU)
+            nc.sync.dma_start(out=out_tiles[c, e], in_=o_sb[:])
+
+        def when_valid(stage, n):
+            if 0 <= n < TILES:
+                stage(n)
+
+        for step in range(-2, TILES + 2):
+            when_valid(project, step - 2)
+            when_valid(aggregate, step)
+            when_valid(add_self, step - 1)
+            when_valid(finish, step - 2)
+            when_valid(quantise_z, step - 1)
+            when_valid(transpose, step + 2)

@@ -22,6 +22,8 @@ PASSES = NODES // (P * PACK)
 PAIR = 2
 CHUNKS = NODES // (P * PAIR)
 TILES = CHUNKS * PAIR
+TRANSPOSE_AHEAD = 4
+QUANTISE_AHEAD = 2
 
 FLOPS = 2 * NODES * NODES * FEAT + 2 * NODES * FEAT * FEAT
 
@@ -30,7 +32,7 @@ def tile_gin_pb_kernel(tc, A, h1, eps1, W1_1_words, W1_1_scales, b1_1, out):
     nc = tc.nc
     with ExitStack() as ctx:
         keep = ctx.enter_context(tc.tile_pool(name="keep", bufs=1))
-        a_pool = ctx.enter_context(tc.tile_pool(name="a_pool", bufs=CHUNKS))
+        a_pool = ctx.enter_context(tc.tile_pool(name="a_pool", bufs=TILES))
         work = ctx.enter_context(tc.tile_pool(name="work", bufs=4))
         psum_t = ctx.enter_context(tc.psum_pool(name="psum_t", bufs=4))
         psum_z = ctx.enter_context(tc.psum_pool(name="psum_z", bufs=2))
@@ -46,10 +48,6 @@ def tile_gin_pb_kernel(tc, A, h1, eps1, W1_1_words, W1_1_scales, b1_1, out):
         ident = keep.tile([P, P], F32)
         make_identity(nc, ident[:])
 
-        nc.sync.dma_start(out=bias_row[0:1, :], in_=b1_1.rearrange("(o n) -> o n", o=1))
-        eps_bc = keep.tile([P, 1], BF16)
-        nc.sync.dma_start(out=eps_bc[:], in_=eps1.partition_broadcast(P))
-
         h1_raw = keep.tile([P, CHUNKS, PAIR, FEAT], BF16)
         h1_rows = h1.rearrange("(c p e) f -> p c (e f)", p=P, e=PAIR)
         for g in range(PASSES):
@@ -57,17 +55,21 @@ def tile_gin_pb_kernel(tc, A, h1, eps1, W1_1_words, W1_1_scales, b1_1, out):
                 out=h1_raw[:, 2 * g : 2 * g + 2].rearrange("p c e f -> p c (e f)"),
                 in_=h1_rows[:, 2 * g : 2 * g + 2, :],
             )
+        eps_bc = keep.tile([P, 1], BF16)
+        nc.sync.dma_start(out=eps_bc[:], in_=eps1.partition_broadcast(P))
+        nc.sync.dma_start(out=bias_row[0:1, :], in_=b1_1.rearrange("(o n) -> o n", o=1))
 
-        a_rows = A.rearrange("(c p e) j -> c p (e j)", p=P, e=PAIR)
+        a_rows = A.rearrange("(c p e) j -> c e p j", p=P, e=PAIR)
         a_tiles = []
 
-        def load_a(c):
-            a_sb = a_pool.tile([P, PAIR, NODES], BF16)
-            nc.sync.dma_start(out=a_sb[:].rearrange("p e j -> p (e j)"), in_=a_rows[c])
+        def load_a(n):
+            c, e = divmod(n, PAIR)
+            a_sb = a_pool.tile([P, NODES], BF16)
+            nc.sync.dma_start(out=a_sb[:], in_=a_rows[c, e])
             a_tiles.append(a_sb)
 
-        load_a(0)
-        load_a(1)
+        for n in range(TILES // 2):
+            load_a(n)
         w_codes = keep.tile([P, FEAT], U32, align_bytes=64)
         nc.sync.dma_start(
             out=w_codes[:].bitcast(I32),
@@ -78,13 +80,8 @@ def tile_gin_pb_kernel(tc, A, h1, eps1, W1_1_words, W1_1_scales, b1_1, out):
                 out=w_plane[32 * quad : 32 * quad + 4, :].bitcast(I32),
                 in_=W1_1_scales[0, 4 * quad : 4 * quad + 4, :].bitcast(I32),
             )
-        load_a(2)
-        load_a(3)
-
-        bias_ps = psum_o.tile([P, FEAT], F32, tag="o_ps")
-        nc.tensor.matmul(bias_ps[:], lhsT=ones[:], rhs=bias_row[:], start=True, stop=True)
-        bias_sb = keep.tile([P, FEAT], F32)
-        nc.scalar.copy(out=bias_sb[:], in_=bias_ps[:])
+        for n in range(TILES // 2, TILES):
+            load_a(n)
 
         h1_grouped = keep.tile([P, PASSES, PACK, P, PACK], BF16, align_bytes=64)
         h1_codes = keep.tile([P, PASSES, FEAT], U32, align_bytes=64)
@@ -105,32 +102,31 @@ def tile_gin_pb_kernel(tc, A, h1, eps1, W1_1_words, W1_1_scales, b1_1, out):
         nc.vector.tensor_scalar_add(self_w[:], eps_bc[:], 1.0)
 
         h1T = keep.tile([P, CHUNKS, PAIR, P, PACK], BF16)
-
+        bias_sb = keep.tile([P, FEAT], F32)
         a_grouped_of = {}
         a_codes_of = {}
         z_ps_of = {}
         z_grouped_of = {}
         z_codes_of = {}
         o_ps_of = {}
+        out_tiles = out.rearrange("(c p e) n -> c e p n", p=P, e=PAIR)
 
-        def transpose(n):
-            if n < CHUNKS:
-                hT_ps = psum_t.tile([P, PAIR, HALF, P], F32, tag="t_ps")
-                for e in range(PAIR):
-                    for u in range(HALF):
-                        nc.tensor.transpose(
-                            hT_ps[:, e, u, :],
-                            h1_raw[:, n, e, :].bitcast(F32)[:, u : FEAT // HALF : HALF],
-                            ident[:],
-                        )
-                nc.scalar.copy(
-                    out=h1T[:, n].bitcast(F32), in_=hT_ps[:].rearrange("m e u i -> m e i u")
-                )
-            c, e = divmod(n, PAIR)
+        def transpose_h1(c):
+            hT_ps = psum_t.tile([P, PAIR, HALF, P], F32, tag="t_ps")
+            for e in range(PAIR):
+                for u in range(HALF):
+                    nc.tensor.transpose(
+                        hT_ps[:, e, u, :],
+                        h1_raw[:, c, e, :].bitcast(F32)[:, u : FEAT // HALF : HALF],
+                        ident[:],
+                    )
+            nc.scalar.copy(out=h1T[:, c].bitcast(F32), in_=hT_ps[:].rearrange("m e u i -> m e i u"))
+
+        def transpose_a(n):
             aT_ps = psum_t.tile([P, PASSES * HALF, P], F32, tag="t_ps")
             for b in range(PASSES * HALF):
                 nc.tensor.transpose(
-                    aT_ps[:, b, :], a_tiles[c][:, e, :].bitcast(F32)[:, P * b : P * (b + 1)], ident[:]
+                    aT_ps[:, b, :], a_tiles[n][:].bitcast(F32)[:, P * b : P * (b + 1)], ident[:]
                 )
             a_grouped = work.tile([P, PASSES, P, PACK], BF16, align_bytes=64)
             nc.scalar.copy(
@@ -139,7 +135,7 @@ def tile_gin_pb_kernel(tc, A, h1, eps1, W1_1_words, W1_1_scales, b1_1, out):
             )
             a_grouped_of[n] = a_grouped
 
-        def aggregate(n):
+        def quantise_a(n):
             a_codes = work.tile([P, PASSES, P], U32, align_bytes=64)
             a_plane = work.tile([P, PASSES, P], U8, align_bytes=64)
             nc.vector.quantize_mx(
@@ -147,6 +143,10 @@ def tile_gin_pb_kernel(tc, A, h1, eps1, W1_1_words, W1_1_scales, b1_1, out):
                 scales=a_plane[:].rearrange("q g i -> q (g i)"),
                 in_=a_grouped_of[n][:].rearrange("q g i t -> q (g i t)"),
             )
+            a_codes_of[n] = (a_codes, a_plane)
+
+        def aggregate(n):
+            a_codes, a_plane = a_codes_of[n]
             z_ps = psum_z.tile([P, PACK, P], F32)
             for s in range(PACK):
                 for g in range(PASSES):
@@ -198,7 +198,10 @@ def tile_gin_pb_kernel(tc, A, h1, eps1, W1_1_words, W1_1_scales, b1_1, out):
             )
             o_ps_of[n] = o_ps
 
-        out_tiles = out.rearrange("(c p e) n -> c e p n", p=P, e=PAIR)
+        def spread_bias():
+            bias_ps = psum_o.tile([P, FEAT], F32, tag="o_ps")
+            nc.tensor.matmul(bias_ps[:], lhsT=ones[:], rhs=bias_row[:], start=True, stop=True)
+            nc.scalar.copy(out=bias_sb[:], in_=bias_ps[:])
 
         def finish(n):
             c, e = divmod(n, PAIR)
@@ -207,14 +210,19 @@ def tile_gin_pb_kernel(tc, A, h1, eps1, W1_1_words, W1_1_scales, b1_1, out):
             nc.scalar.activation(out=o_sb[:], in_=o_sb[:], func=RELU)
             nc.sync.dma_start(out=out_tiles[c, e], in_=o_sb[:])
 
-        def when_valid(stage, n):
-            if 0 <= n < TILES:
-                stage(n)
+        def run(stage, index, count):
+            if 0 <= index < count:
+                stage(index)
 
-        for step in range(-2, TILES + 2):
-            when_valid(project, step - 2)
-            when_valid(aggregate, step)
-            when_valid(add_self, step - 1)
-            when_valid(finish, step - 2)
-            when_valid(quantise_z, step - 1)
-            when_valid(transpose, step + 2)
+        for c in range(CHUNKS):
+            transpose_h1(c)
+        for step in range(-TRANSPOSE_AHEAD, TILES + 2):
+            run(project, step - 2, TILES)
+            run(aggregate, step, TILES)
+            run(add_self, step - 1, TILES)
+            run(quantise_a, step + QUANTISE_AHEAD, TILES)
+            run(quantise_z, step - 1, TILES)
+            run(transpose_a, step + TRANSPOSE_AHEAD, TILES)
+            if step == -1:
+                spread_bias()
+            run(finish, step - 2, TILES)

@@ -216,13 +216,13 @@ def tile_gin_pb_kernel(tc, A, h1, eps1, W1_1_words, W1_1_scales, b1_1, out):
 
         for c in range(CHUNKS):
             transpose_h1(c)
-        for step in range(-TRANSPOSE_AHEAD, TILES + 2):
-            run(project, step - 2, TILES)
+        for step in range(-TRANSPOSE_AHEAD, TILES + 3):
+            run(project, step - 3, TILES)
             run(aggregate, step, TILES)
+            run(quantise_z, step - 2, TILES)
             run(add_self, step - 1, TILES)
             run(quantise_a, step + QUANTISE_AHEAD, TILES)
-            run(quantise_z, step - 1, TILES)
             run(transpose_a, step + TRANSPOSE_AHEAD, TILES)
             if step == -1:
                 spread_bias()
-            run(finish, step - 2, TILES)
+            run(finish, step - 3, TILES)

@@ -214,14 +214,15 @@ def tile_gin_pb_kernel(tc, A, h1, eps1, W1_1_words, W1_1_scales, b1_1, out):
             if 0 <= index < count:
                 stage(index)
 
-        for c in range(CHUNKS):
-            transpose_h1(c)
+        transpose_h1(0)
         for step in range(-TRANSPOSE_AHEAD, TILES + 3):
             run(project, step - 3, TILES)
             run(aggregate, step, TILES)
             run(quantise_z, step - 2, TILES)
             run(add_self, step - 1, TILES)
             run(quantise_a, step + QUANTISE_AHEAD, TILES)
+            if step >= 0 and step % PAIR == 0:
+                run(transpose_h1, step // PAIR + 1, CHUNKS)
             run(transpose_a, step + TRANSPOSE_AHEAD, TILES)
             if step == -1:
                 spread_bias()

@@ -24,6 +24,7 @@ CHUNKS = NODES // (P * PAIR)
 TILES = CHUNKS * PAIR
 TRANSPOSE_AHEAD = 4
 QUANTISE_AHEAD = 2
+VECTOR_WORDS = 80
 
 FLOPS = 2 * NODES * NODES * FEAT + 2 * NODES * FEAT * FEAT
 
@@ -34,6 +35,7 @@ def tile_gin_pb_kernel(tc, A, h1, eps1, W1_1_words, W1_1_scales, b1_1, out):
         keep = ctx.enter_context(tc.tile_pool(name="keep", bufs=1))
         a_pool = ctx.enter_context(tc.tile_pool(name="a_pool", bufs=TILES))
         work = ctx.enter_context(tc.tile_pool(name="work", bufs=4))
+        out_pool = ctx.enter_context(tc.tile_pool(name="out_pool", bufs=TILES))
         psum_t = ctx.enter_context(tc.psum_pool(name="psum_t", bufs=4))
         psum_z = ctx.enter_context(tc.psum_pool(name="psum_z", bufs=2))
         psum_o = ctx.enter_context(tc.psum_pool(name="psum_o", bufs=2))
@@ -87,10 +89,10 @@ def tile_gin_pb_kernel(tc, A, h1, eps1, W1_1_words, W1_1_scales, b1_1, out):
         h1_codes = keep.tile([P, PASSES, FEAT], U32, align_bytes=64)
         h1_plane = keep.tile([P, PASSES, FEAT], U8, align_bytes=64)
         for g in range(PASSES):
-            nc.vector.tensor_copy(
-                out=h1_grouped[:, g].rearrange("q s m t -> q m s t"),
-                in_=h1_raw[:, 2 * g : 2 * g + 2].rearrange("q c e (m s) -> q m s (c e)", s=PACK),
-            )
+            grouped = h1_grouped[:, g].rearrange("q s m t -> q m s t")
+            raw = h1_raw[:, 2 * g : 2 * g + 2].rearrange("q c e (m s) -> q m s (c e)", s=PACK)
+            nc.vector.tensor_copy(out=grouped[:, :VECTOR_WORDS], in_=raw[:, :VECTOR_WORDS])
+            nc.scalar.copy(out=grouped[:, VECTOR_WORDS:], in_=raw[:, VECTOR_WORDS:])
         for g in range(PASSES):
             nc.vector.quantize_mx(
                 out=h1_codes[:, g, :].bitcast(FP8X4),
@@ -205,7 +207,7 @@ def tile_gin_pb_kernel(tc, A, h1, eps1, W1_1_words, W1_1_scales, b1_1, out):
 
         def finish(n):
             c, e = divmod(n, PAIR)
-            o_sb = work.tile([P, FEAT], F32)
+            o_sb = out_pool.tile([P, FEAT], F32)
             nc.vector.tensor_tensor(out=o_sb[:], in0=o_ps_of[n][:], in1=bias_sb[:], op=ADD)
             nc.scalar.activation(out=o_sb[:], in_=o_sb[:], func=RELU)
             nc.sync.dma_start(out=out_tiles[c, e], in_=o_sb[:])

@@ -43,6 +43,8 @@ def tile_gin_pb_kernel(tc, A, h1, eps1, W1_1_words, W1_1_scales, b1_1, out):
 
         bias_row = keep.tile([P, FEAT], BF16)
         nc.vector.memset(bias_row[:], 0.0)
+        eps_row = keep.tile([P, HALF], BF16)
+        nc.vector.memset(eps_row[:], 0.0)
         w_plane = keep.tile([P, FEAT], U8, align_bytes=64)
         nc.vector.memset(w_plane[:].bitcast(I32), 0)
         ones = keep.tile([P, P], BF16)
@@ -57,8 +59,7 @@ def tile_gin_pb_kernel(tc, A, h1, eps1, W1_1_words, W1_1_scales, b1_1, out):
                 out=h1_raw[:, 2 * g : 2 * g + 2].rearrange("p c e f -> p c (e f)"),
                 in_=h1_rows[:, 2 * g : 2 * g + 2, :],
             )
-        eps_bc = keep.tile([P, 1], BF16)
-        nc.sync.dma_start(out=eps_bc[:], in_=eps1.partition_broadcast(P))
+        nc.sync.dma_start(out=eps_row[0:1, 0:1], in_=eps1.rearrange("(o n) -> o n", o=1))
         nc.sync.dma_start(out=bias_row[0:1, :], in_=b1_1.rearrange("(o n) -> o n", o=1))
 
         a_rows = A.rearrange("(c p e) j -> c e p j", p=P, e=PAIR)
@@ -101,7 +102,6 @@ def tile_gin_pb_kernel(tc, A, h1, eps1, W1_1_words, W1_1_scales, b1_1, out):
             )
 
         self_w = keep.tile([P, 1], F32)
-        nc.vector.tensor_scalar_add(self_w[:], eps_bc[:], 1.0)
 
         h1T = keep.tile([P, CHUNKS, PAIR, P, PACK], BF16)
         bias_sb = keep.tile([P, FEAT], F32)
@@ -200,7 +200,10 @@ def tile_gin_pb_kernel(tc, A, h1, eps1, W1_1_words, W1_1_scales, b1_1, out):
             )
             o_ps_of[n] = o_ps
 
-        def spread_bias():
+        def spread_rows():
+            eps_ps = psum_o.tile([P, HALF], F32, tag="o_ps")
+            nc.tensor.matmul(eps_ps[:], lhsT=ones[:], rhs=eps_row[:], start=True, stop=True)
+            nc.vector.tensor_scalar_add(self_w[:], eps_ps[:, 0:1], 1.0)
             bias_ps = psum_o.tile([P, FEAT], F32, tag="o_ps")
             nc.tensor.matmul(bias_ps[:], lhsT=ones[:], rhs=bias_row[:], start=True, stop=True)
             nc.scalar.copy(out=bias_sb[:], in_=bias_ps[:])
@@ -227,5 +230,5 @@ def tile_gin_pb_kernel(tc, A, h1, eps1, W1_1_words, W1_1_scales, b1_1, out):
                 run(transpose_h1, step // PAIR + 1, CHUNKS)
             run(transpose_a, step + TRANSPOSE_AHEAD, TILES)
             if step == -1:
-                spread_bias()
+                spread_rows()
             run(finish, step - 3, TILES)

@@ -210,10 +210,15 @@ def tile_gin_pb_kernel(tc, A, h1, eps1, W1_1_words, W1_1_scales, b1_1, out):
 
         def finish(n):
             c, e = divmod(n, PAIR)
-            o_sb = out_pool.tile([P, FEAT], F32)
-            nc.vector.tensor_tensor(out=o_sb[:], in0=o_ps_of[n][:], in1=bias_sb[:], op=ADD)
-            nc.scalar.activation(out=o_sb[:], in_=o_sb[:], func=RELU)
-            nc.sync.dma_start(out=out_tiles[c, e], in_=o_sb[:])
+            width = FEAT // 2 if n == TILES - 1 else FEAT
+            for lo in range(0, FEAT, width):
+                cols = slice(lo, lo + width)
+                o_sb = out_pool.tile([P, width], F32)
+                nc.vector.tensor_tensor(
+                    out=o_sb[:], in0=o_ps_of[n][:, cols], in1=bias_sb[:, cols], op=ADD
+                )
+                nc.scalar.activation(out=o_sb[:], in_=o_sb[:], func=RELU)
+                nc.sync.dma_start(out=out_tiles[c, e, :, cols], in_=o_sb[:])
 
         def run(stage, index, count):
             if 0 <= index < count:
@@ -226,9 +231,12 @@ def tile_gin_pb_kernel(tc, A, h1, eps1, W1_1_words, W1_1_scales, b1_1, out):
             run(quantise_z, step - 2, TILES)
             run(add_self, step - 1, TILES)
             run(quantise_a, step + QUANTISE_AHEAD, TILES)
-            if step >= 0 and step % PAIR == 0:
-                run(transpose_h1, step // PAIR + 1, CHUNKS)
-            run(transpose_a, step + TRANSPOSE_AHEAD, TILES)
+            if step < 0:
+                transpose_a(step + TRANSPOSE_AHEAD)
+            if step > 0:
+                run(transpose_a, step + TRANSPOSE_AHEAD - 1, TILES)
+                if step % PAIR == 1:
+                    run(transpose_h1, (step + 1) // PAIR, CHUNKS)
             if step == -1:
                 spread_rows()
             run(finish, step - 3, TILES)

@@ -24,6 +24,8 @@ CHUNKS = NODES // (P * PAIR)
 TILES = CHUNKS * PAIR
 TRANSPOSE_AHEAD = 4
 QUANTISE_AHEAD = 2
+WARM_BEFORE = 4
+WARM_BETWEEN = 2
 VECTOR_WORDS = 80
 
 FLOPS = 2 * NODES * NODES * FEAT + 2 * NODES * FEAT * FEAT
@@ -41,14 +43,16 @@ def tile_gin_pb_kernel(tc, A, h1, eps1, W1_1_words, W1_1_scales, b1_1, out):
         psum_o = ctx.enter_context(tc.psum_pool(name="psum_o", bufs=2))
         ctx.enter_context(tc.manual_schedule())
 
+        ones = keep.tile([P, P], BF16)
+        nc.vector.memset(ones[:], 1.0)
+        warm_row = keep.tile([P, FEAT], BF16)
+        nc.vector.memset(warm_row[:], 0.0)
         bias_row = keep.tile([P, FEAT], BF16)
         nc.vector.memset(bias_row[:], 0.0)
         eps_row = keep.tile([P, HALF], BF16)
         nc.vector.memset(eps_row[:], 0.0)
         w_plane = keep.tile([P, FEAT], U8, align_bytes=64)
         nc.vector.memset(w_plane[:].bitcast(I32), 0)
-        ones = keep.tile([P, P], BF16)
-        nc.vector.memset(ones[:], 1.0)
         ident = keep.tile([P, P], F32)
         make_identity(nc, ident[:])
 
@@ -200,6 +204,11 @@ def tile_gin_pb_kernel(tc, A, h1, eps1, W1_1_words, W1_1_scales, b1_1, out):
             )
             o_ps_of[n] = o_ps
 
+        def warm_up(count):
+            warm_ps = psum_o.tile([P, FEAT], F32, tag="o_ps")
+            for rep in range(count):
+                nc.tensor.matmul(warm_ps[:], lhsT=ones[:], rhs=warm_row[:], start=True, stop=True)
+
         def spread_rows():
             eps_ps = psum_o.tile([P, HALF], F32, tag="o_ps")
             nc.tensor.matmul(eps_ps[:], lhsT=ones[:], rhs=eps_row[:], start=True, stop=True)
@@ -224,7 +233,9 @@ def tile_gin_pb_kernel(tc, A, h1, eps1, W1_1_words, W1_1_scales, b1_1, out):
             if 0 <= index < count:
                 stage(index)
 
+        warm_up(WARM_BEFORE)
         transpose_h1(0)
+        warm_up(WARM_BETWEEN)
         for step in range(-TRANSPOSE_AHEAD, TILES + 3):
             run(project, step - 3, TILES)
             run(aggregate, step, TILES)
@@ -233,6 +244,8 @@ def tile_gin_pb_kernel(tc, A, h1, eps1, W1_1_words, W1_1_scales, b1_1, out):
             run(quantise_a, step + QUANTISE_AHEAD, TILES)
             if step < 0:
                 transpose_a(step + TRANSPOSE_AHEAD)
+                if step < -PAIR:
+                    warm_up(1)
             if step > 0:
                 run(transpose_a, step + TRANSPOSE_AHEAD - 1, TILES)
                 if step % PAIR == 1:

@@ -25,8 +25,7 @@ TILES = CHUNKS * PAIR
 TRANSPOSE_AHEAD = 4
 QUANTISE_AHEAD = 2
 WARM_BEFORE = 4
-WARM_BETWEEN = 2
-VECTOR_WORDS = 80
+VECTOR_WORDS = 96
 
 FLOPS = 2 * NODES * NODES * FEAT + 2 * NODES * FEAT * FEAT
 
@@ -209,6 +208,18 @@ def tile_gin_pb_kernel(tc, A, h1, eps1, W1_1_words, W1_1_scales, b1_1, out):
             for rep in range(count):
                 nc.tensor.matmul(warm_ps[:], lhsT=ones[:], rhs=warm_row[:], start=True, stop=True)
 
+        def keep_warm():
+            idle_ps = psum_z.tile([P, FEAT], F32, tag="z_ps")
+            nc.tensor.matmul_mx(
+                out=idle_ps[:],
+                lhsT=h1_codes[:, 0, :P].bitcast(FP8X4),
+                lhsT_scale=h1_plane[:, 0, :P],
+                rhs=h1_codes[:, 0, :].bitcast(FP8X4),
+                rhs_scale=h1_plane[:, 0, :],
+                start=True,
+                stop=True,
+            )
+
         def spread_rows():
             eps_ps = psum_o.tile([P, HALF], F32, tag="o_ps")
             nc.tensor.matmul(eps_ps[:], lhsT=ones[:], rhs=eps_row[:], start=True, stop=True)
@@ -234,11 +245,14 @@ def tile_gin_pb_kernel(tc, A, h1, eps1, W1_1_words, W1_1_scales, b1_1, out):
                 stage(index)
 
         warm_up(WARM_BEFORE)
-        transpose_h1(0)
-        warm_up(WARM_BETWEEN)
+        for c in range(CHUNKS // 2):
+            transpose_h1(c)
+            warm_up(1)
         for step in range(-TRANSPOSE_AHEAD, TILES + 3):
             run(project, step - 3, TILES)
             run(aggregate, step, TILES)
+            if TILES <= step < TILES + 2:
+                keep_warm()
             run(quantise_z, step - 2, TILES)
             run(add_self, step - 1, TILES)
             run(quantise_a, step + QUANTISE_AHEAD, TILES)
@@ -246,9 +260,10 @@ def tile_gin_pb_kernel(tc, A, h1, eps1, W1_1_words, W1_1_scales, b1_1, out):
                 transpose_a(step + TRANSPOSE_AHEAD)
                 if step < -PAIR:
                     warm_up(1)
-            if step > 0:
+            elif step % PAIR == 1:
                 run(transpose_a, step + TRANSPOSE_AHEAD - 1, TILES)
-                if step % PAIR == 1:
+                run(transpose_a, step + TRANSPOSE_AHEAD, TILES)
+                if step > 1:
                     run(transpose_h1, (step + 1) // PAIR, CHUNKS)
             if step == -1:
                 spread_rows()

@@ -25,6 +25,7 @@ TILES = CHUNKS * PAIR
 TRANSPOSE_AHEAD = 4
 QUANTISE_AHEAD = 2
 WARM_BEFORE = 4
+LOADS_BEFORE_W = 6
 VECTOR_WORDS = 96
 
 FLOPS = 2 * NODES * NODES * FEAT + 2 * NODES * FEAT * FEAT
@@ -74,7 +75,7 @@ def tile_gin_pb_kernel(tc, A, h1, eps1, W1_1_words, W1_1_scales, b1_1, out):
             nc.sync.dma_start(out=a_sb[:], in_=a_rows[c, e])
             a_tiles.append(a_sb)
 
-        for n in range(TILES // 2):
+        for n in range(LOADS_BEFORE_W):
             load_a(n)
         w_codes = keep.tile([P, FEAT], U32, align_bytes=64)
         nc.sync.dma_start(
@@ -86,7 +87,7 @@ def tile_gin_pb_kernel(tc, A, h1, eps1, W1_1_words, W1_1_scales, b1_1, out):
                 out=w_plane[32 * quad : 32 * quad + 4, :].bitcast(I32),
                 in_=W1_1_scales[0, 4 * quad : 4 * quad + 4, :].bitcast(I32),
             )
-        for n in range(TILES // 2, TILES):
+        for n in range(LOADS_BEFORE_W, TILES):
             load_a(n)
 
         h1_grouped = keep.tile([P, PASSES, PACK, P, PACK], BF16, align_bytes=64)

@@ -26,6 +26,7 @@ TRANSPOSE_AHEAD = 4
 QUANTISE_AHEAD = 2
 WARM_BEFORE = 4
 LOADS_BEFORE_W = 6
+SCALAR_TILES = (3,)
 VECTOR_WORDS = 96
 
 FLOPS = 2 * NODES * NODES * FEAT + 2 * NODES * FEAT * FEAT
@@ -109,12 +110,14 @@ def tile_gin_pb_kernel(tc, A, h1, eps1, W1_1_words, W1_1_scales, b1_1, out):
 
         h1T = keep.tile([P, CHUNKS, PAIR, P, PACK], BF16)
         bias_sb = keep.tile([P, FEAT], F32)
+        bias_col = keep.tile([P, PACK], F32)
         a_grouped_of = {}
         a_codes_of = {}
         z_ps_of = {}
         z_grouped_of = {}
         z_codes_of = {}
         o_ps_of = {}
+        oT_of = {}
         out_tiles = out.rearrange("(c p e) n -> c e p n", p=P, e=PAIR)
 
         def transpose_h1(c):
@@ -229,6 +232,18 @@ def tile_gin_pb_kernel(tc, A, h1, eps1, W1_1_words, W1_1_scales, b1_1, out):
             nc.tensor.matmul(bias_ps[:], lhsT=ones[:], rhs=bias_row[:], start=True, stop=True)
             nc.scalar.copy(out=bias_sb[:], in_=bias_ps[:])
 
+        def spread_bias_cols():
+            col_ps = psum_z.tile([P, PACK, HALF], F32, tag="z_ps")
+            for j in range(PACK):
+                nc.tensor.matmul(
+                    col_ps[:, j, :],
+                    lhsT=bias_row[:, P * j : P * (j + 1)],
+                    rhs=ones[:, 0:HALF],
+                    start=True,
+                    stop=True,
+                )
+            nc.scalar.copy(out=bias_col[:], in_=col_ps[:, :, 0])
+
         def finish(n):
             c, e = divmod(n, PAIR)
             width = FEAT // 2 if n == TILES - 1 else FEAT
@@ -241,6 +256,35 @@ def tile_gin_pb_kernel(tc, A, h1, eps1, W1_1_words, W1_1_scales, b1_1, out):
                 nc.scalar.activation(out=o_sb[:], in_=o_sb[:], func=RELU)
                 nc.sync.dma_start(out=out_tiles[c, e, :, cols], in_=o_sb[:])
 
+        def project_T(n):
+            z_codes, z_plane = z_codes_of[n]
+            oT_ps = psum_o.tile([P, PACK, P], F32, tag="o_ps")
+            for j in range(PACK):
+                nc.tensor.matmul_mx(
+                    out=oT_ps[:, j, :],
+                    lhsT=w_codes[:, P * j : P * (j + 1)].bitcast(FP8X4),
+                    lhsT_scale=w_plane[:, P * j : P * (j + 1)],
+                    rhs=z_codes[:].bitcast(FP8X4),
+                    rhs_scale=z_plane[:],
+                    start=True,
+                    stop=True,
+                )
+            oT_sb = work.tile([P, PACK, P], F32)
+            for j in range(PACK):
+                nc.scalar.activation(
+                    out=oT_sb[:, j, :], in_=oT_ps[:, j, :], func=RELU, bias=bias_col[:, j : j + 1]
+                )
+            oT_of[n] = oT_sb
+
+        def turn_back(n):
+            c, e = divmod(n, PAIR)
+            turn_ps = psum_t.tile([P, PACK, P], F32, tag="t_ps")
+            for j in range(PACK):
+                nc.tensor.transpose(turn_ps[:, j, :], oT_of[n][:, j, :], ident[:])
+            o_sb = out_pool.tile([P, FEAT], F32)
+            nc.scalar.copy(out=o_sb[:], in_=turn_ps[:].rearrange("i j p -> i (j p)"))
+            nc.sync.dma_start(out=out_tiles[c, e], in_=o_sb[:])
+
         def run(stage, index, count):
             if 0 <= index < count:
                 stage(index)
@@ -249,8 +293,12 @@ def tile_gin_pb_kernel(tc, A, h1, eps1, W1_1_words, W1_1_scales, b1_1, out):
         for c in range(CHUNKS // 2):
             transpose_h1(c)
             warm_up(1)
+        spread_bias_cols()
         for step in range(-TRANSPOSE_AHEAD, TILES + 3):
-            run(project, step - 3, TILES)
+            if step - 3 in SCALAR_TILES:
+                project_T(step - 3)
+            else:
+                run(project, step - 3, TILES)
             run(aggregate, step, TILES)
             if TILES <= step < TILES + 2:
                 keep_warm()
@@ -268,4 +316,7 @@ def tile_gin_pb_kernel(tc, A, h1, eps1, W1_1_words, W1_1_scales, b1_1, out):
                     run(transpose_h1, (step + 1) // PAIR, CHUNKS)
             if step == -1:
                 spread_rows()
-            run(finish, step - 3, TILES)
+            if step - 4 in SCALAR_TILES:
+                turn_back(step - 4)
+            if step - 3 not in SCALAR_TILES:
+                run(finish, step - 3, TILES)

from contextlib import ExitStack

import concourse.mybir as mybir
from concourse.masks import make_identity

F32 = mybir.dt.float32
BF16 = mybir.dt.bfloat16
I32 = mybir.dt.int32
U32 = mybir.dt.uint32
U8 = mybir.dt.uint8
FP8X4 = mybir.dt.float8_e4m3fn_x4
ADD = mybir.AluOpType.add
MULT = mybir.AluOpType.mult
RELU = mybir.ActivationFunctionType.Relu

P = 128
PACK = 4
HALF = 2
NODES = 1024
FEAT = 512
PASSES = NODES // (P * PACK)
PAIR = 2
CHUNKS = NODES // (P * PAIR)
TILES = CHUNKS * PAIR
TRANSPOSE_AHEAD = 4
QUANTISE_AHEAD = 2
WARM_BEFORE = 4
LOADS_BEFORE_W = 6
SCALAR_TILES = (3,)
VECTOR_WORDS = 96

FLOPS = 2 * NODES * NODES * FEAT + 2 * NODES * FEAT * FEAT


def tile_gin_pb_kernel(tc, A, h1, eps1, W1_1_words, W1_1_scales, b1_1, out):
    nc = tc.nc
    with ExitStack() as ctx:
        keep = ctx.enter_context(tc.tile_pool(name="keep", bufs=1))
        a_pool = ctx.enter_context(tc.tile_pool(name="a_pool", bufs=TILES))
        work = ctx.enter_context(tc.tile_pool(name="work", bufs=4))
        out_pool = ctx.enter_context(tc.tile_pool(name="out_pool", bufs=TILES))
        psum_t = ctx.enter_context(tc.psum_pool(name="psum_t", bufs=4))
        psum_z = ctx.enter_context(tc.psum_pool(name="psum_z", bufs=2))
        psum_o = ctx.enter_context(tc.psum_pool(name="psum_o", bufs=2))
        ctx.enter_context(tc.manual_schedule())

        ones = keep.tile([P, P], BF16)
        nc.vector.memset(ones[:], 1.0)
        warm_row = keep.tile([P, FEAT], BF16)
        nc.vector.memset(warm_row[:], 0.0)
        bias_row = keep.tile([P, FEAT], BF16)
        nc.vector.memset(bias_row[:], 0.0)
        eps_row = keep.tile([P, HALF], BF16)
        nc.vector.memset(eps_row[:], 0.0)
        w_plane = keep.tile([P, FEAT], U8, align_bytes=64)
        nc.vector.memset(w_plane[:].bitcast(I32), 0)
        ident = keep.tile([P, P], F32)
        make_identity(nc, ident[:])

        h1_raw = keep.tile([P, CHUNKS, PAIR, FEAT], BF16)
        h1_rows = h1.rearrange("(c p e) f -> p c (e f)", p=P, e=PAIR)
        for g in range(PASSES):
            nc.sync.dma_start(
                out=h1_raw[:, 2 * g : 2 * g + 2].rearrange("p c e f -> p c (e f)"),
                in_=h1_rows[:, 2 * g : 2 * g + 2, :],
            )
        nc.sync.dma_start(out=eps_row[0:1, 0:1], in_=eps1.rearrange("(o n) -> o n", o=1))
        nc.sync.dma_start(out=bias_row[0:1, :], in_=b1_1.rearrange("(o n) -> o n", o=1))

        a_rows = A.rearrange("(c p e) j -> c e p j", p=P, e=PAIR)
        a_tiles = []

        def load_a(n):
            c, e = divmod(n, PAIR)
            a_sb = a_pool.tile([P, NODES], BF16)
            nc.sync.dma_start(out=a_sb[:], in_=a_rows[c, e])
            a_tiles.append(a_sb)

        for n in range(LOADS_BEFORE_W):
            load_a(n)
        w_codes = keep.tile([P, FEAT], U32, align_bytes=64)
        nc.sync.dma_start(
            out=w_codes[:].bitcast(I32),
            in_=W1_1_words[0].rearrange("p n t -> p (n t)").bitcast(I32),
        )
        for quad in range(4):
            nc.sync.dma_start(
                out=w_plane[32 * quad : 32 * quad + 4, :].bitcast(I32),
                in_=W1_1_scales[0, 4 * quad : 4 * quad + 4, :].bitcast(I32),
            )
        for n in range(LOADS_BEFORE_W, TILES):
            load_a(n)

        h1_grouped = keep.tile([P, PASSES, PACK, P, PACK], BF16, align_bytes=64)
        h1_codes = keep.tile([P, PASSES, FEAT], U32, align_bytes=64)
        h1_plane = keep.tile([P, PASSES, FEAT], U8, align_bytes=64)
        for g in range(PASSES):
            grouped = h1_grouped[:, g].rearrange("q s m t -> q m s t")
            raw = h1_raw[:, 2 * g : 2 * g + 2].rearrange("q c e (m s) -> q m s (c e)", s=PACK)
            nc.vector.tensor_copy(out=grouped[:, :VECTOR_WORDS], in_=raw[:, :VECTOR_WORDS])
            nc.scalar.copy(out=grouped[:, VECTOR_WORDS:], in_=raw[:, VECTOR_WORDS:])
        for g in range(PASSES):
            nc.vector.quantize_mx(
                out=h1_codes[:, g, :].bitcast(FP8X4),
                scales=h1_plane[:, g, :],
                in_=h1_grouped[:, g].rearrange("q s m t -> q (s m t)"),
            )

        self_w = keep.tile([P, 1], F32)

        h1T = keep.tile([P, CHUNKS, PAIR, P, PACK], BF16)
        bias_sb = keep.tile([P, FEAT], F32)
        bias_col = keep.tile([P, PACK], F32)
        a_grouped_of = {}
        a_codes_of = {}
        z_ps_of = {}
        z_grouped_of = {}
        z_codes_of = {}
        o_ps_of = {}
        oT_of = {}
        out_tiles = out.rearrange("(c p e) n -> c e p n", p=P, e=PAIR)

        def transpose_h1(c):
            hT_ps = psum_t.tile([P, PAIR, HALF, P], F32, tag="t_ps")
            for e in range(PAIR):
                for u in range(HALF):
                    nc.tensor.transpose(
                        hT_ps[:, e, u, :],
                        h1_raw[:, c, e, :].bitcast(F32)[:, u : FEAT // HALF : HALF],
                        ident[:],
                    )
            nc.scalar.copy(out=h1T[:, c].bitcast(F32), in_=hT_ps[:].rearrange("m e u i -> m e i u"))

        def transpose_a(n):
            aT_ps = psum_t.tile([P, PASSES * HALF, P], F32, tag="t_ps")
            for b in range(PASSES * HALF):
                nc.tensor.transpose(
                    aT_ps[:, b, :], a_tiles[n][:].bitcast(F32)[:, P * b : P * (b + 1)], ident[:]
                )
            a_grouped = work.tile([P, PASSES, P, PACK], BF16, align_bytes=64)
            nc.scalar.copy(
                out=a_grouped[:].bitcast(F32),
                in_=aT_ps[:].rearrange("q (g u) i -> q g i u", u=HALF),
            )
            a_grouped_of[n] = a_grouped

        def quantise_a(n):
            a_codes = work.tile([P, PASSES, P], U32, align_bytes=64)
            a_plane = work.tile([P, PASSES, P], U8, align_bytes=64)
            nc.vector.quantize_mx(
                out=a_codes[:].rearrange("q g i -> q (g i)").bitcast(FP8X4),
                scales=a_plane[:].rearrange("q g i -> q (g i)"),
                in_=a_grouped_of[n][:].rearrange("q g i t -> q (g i t)"),
            )
            a_codes_of[n] = (a_codes, a_plane)

        def aggregate(n):
            a_codes, a_plane = a_codes_of[n]
            z_ps = psum_z.tile([P, PACK, P], F32)
            for s in range(PACK):
                for g in range(PASSES):
                    nc.tensor.matmul_mx(
                        out=z_ps[:, s, :],
                        lhsT=h1_codes[:, g, P * s : P * (s + 1)].bitcast(FP8X4),
                        lhsT_scale=h1_plane[:, g, P * s : P * (s + 1)],
                        rhs=a_codes[:, g, :].bitcast(FP8X4),
                        rhs_scale=a_plane[:, g, :],
                        start=(g == 0),
                        stop=(g == PASSES - 1),
                    )
            z_ps_of[n] = z_ps

        def add_self(n):
            c, e = divmod(n, PAIR)
            z_grouped = work.tile([P, P, PACK], BF16, align_bytes=64)
            nc.vector.scalar_tensor_tensor(
                out=z_grouped[:],
                in0=h1T[:, c, e],
                scalar=self_w[:, 0:1],
                in1=z_ps_of[n][:].rearrange("m s i -> m i s"),
                op0=MULT,
                op1=ADD,
            )
            z_grouped_of[n] = z_grouped

        def quantise_z(n):
            z_codes = work.tile([P, P], U32, align_bytes=64)
            z_plane = work.tile([P, P], U8, align_bytes=64)
            nc.vector.quantize_mx(
                out=z_codes[:].bitcast(FP8X4),
                scales=z_plane[:],
                in_=z_grouped_of[n][:].rearrange("m i s -> m (i s)"),
            )
            z_codes_of[n] = (z_codes, z_plane)

        def project(n):
            z_codes, z_plane = z_codes_of[n]
            o_ps = psum_o.tile([P, FEAT], F32)
            nc.tensor.matmul_mx(
                out=o_ps[:],
                lhsT=z_codes[:].bitcast(FP8X4),
                lhsT_scale=z_plane[:],
                rhs=w_codes[:].bitcast(FP8X4),
                rhs_scale=w_plane[:],
                start=True,
                stop=True,
            )
            o_ps_of[n] = o_ps

        def warm_up(count):
            warm_ps = psum_o.tile([P, FEAT], F32, tag="o_ps")
            for rep in range(count):
                nc.tensor.matmul(warm_ps[:], lhsT=ones[:], rhs=warm_row[:], start=True, stop=True)

        def keep_warm():
            idle_ps = psum_z.tile([P, FEAT], F32, tag="z_ps")
            nc.tensor.matmul_mx(
                out=idle_ps[:],
                lhsT=h1_codes[:, 0, :P].bitcast(FP8X4),
                lhsT_scale=h1_plane[:, 0, :P],
                rhs=h1_codes[:, 0, :].bitcast(FP8X4),
                rhs_scale=h1_plane[:, 0, :],
                start=True,
                stop=True,
            )

        def spread_rows():
            eps_ps = psum_o.tile([P, HALF], F32, tag="o_ps")
            nc.tensor.matmul(eps_ps[:], lhsT=ones[:], rhs=eps_row[:], start=True, stop=True)
            nc.vector.tensor_scalar_add(self_w[:], eps_ps[:, 0:1], 1.0)
            bias_ps = psum_o.tile([P, FEAT], F32, tag="o_ps")
            nc.tensor.matmul(bias_ps[:], lhsT=ones[:], rhs=bias_row[:], start=True, stop=True)
            nc.scalar.copy(out=bias_sb[:], in_=bias_ps[:])

        def spread_bias_cols():
            col_ps = psum_z.tile([P, PACK, HALF], F32, tag="z_ps")
            for j in range(PACK):
                nc.tensor.matmul(
                    col_ps[:, j, :],
                    lhsT=bias_row[:, P * j : P * (j + 1)],
                    rhs=ones[:, 0:HALF],
                    start=True,
                    stop=True,
                )
            nc.scalar.copy(out=bias_col[:], in_=col_ps[:, :, 0])

        def finish(n):
            c, e = divmod(n, PAIR)
            width = FEAT // 2 if n == TILES - 1 else FEAT
            for lo in range(0, FEAT, width):
                cols = slice(lo, lo + width)
                o_sb = out_pool.tile([P, width], F32)
                nc.vector.tensor_tensor(
                    out=o_sb[:], in0=o_ps_of[n][:, cols], in1=bias_sb[:, cols], op=ADD
                )
                nc.scalar.activation(out=o_sb[:], in_=o_sb[:], func=RELU)
                nc.sync.dma_start(out=out_tiles[c, e, :, cols], in_=o_sb[:])

        def project_T(n):
            z_codes, z_plane = z_codes_of[n]
            oT_ps = psum_o.tile([P, PACK, P], F32, tag="o_ps")
            for j in range(PACK):
                nc.tensor.matmul_mx(
                    out=oT_ps[:, j, :],
                    lhsT=w_codes[:, P * j : P * (j + 1)].bitcast(FP8X4),
                    lhsT_scale=w_plane[:, P * j : P * (j + 1)],
                    rhs=z_codes[:].bitcast(FP8X4),
                    rhs_scale=z_plane[:],
                    start=True,
                    stop=True,
                )
            oT_sb = work.tile([P, PACK, P], F32)
            for j in range(PACK):
                nc.scalar.activation(
                    out=oT_sb[:, j, :], in_=oT_ps[:, j, :], func=RELU, bias=bias_col[:, j : j + 1]
                )
            oT_of[n] = oT_sb

        def turn_back(n):
            c, e = divmod(n, PAIR)
            turn_ps = psum_t.tile([P, PACK, P], F32, tag="t_ps")
            for j in range(PACK):
                nc.tensor.transpose(turn_ps[:, j, :], oT_of[n][:, j, :], ident[:])
            o_sb = out_pool.tile([P, FEAT], F32)
            nc.scalar.copy(out=o_sb[:], in_=turn_ps[:].rearrange("i j p -> i (j p)"))
            nc.sync.dma_start(out=out_tiles[c, e], in_=o_sb[:])

        def run(stage, index, count):
            if 0 <= index < count:
                stage(index)

        warm_up(WARM_BEFORE)
        for c in range(CHUNKS // 2):
            transpose_h1(c)
            warm_up(1)
        spread_bias_cols()
        for step in range(-TRANSPOSE_AHEAD, TILES + 3):
            if step - 3 in SCALAR_TILES:
                project_T(step - 3)
            else:
                run(project, step - 3, TILES)
            run(aggregate, step, TILES)
            if TILES <= step < TILES + 2:
                keep_warm()
            run(quantise_z, step - 2, TILES)
            run(add_self, step - 1, TILES)
            run(quantise_a, step + QUANTISE_AHEAD, TILES)
            if step < 0:
                transpose_a(step + TRANSPOSE_AHEAD)
                if step < -PAIR:
                    warm_up(1)
            elif step % PAIR == 1:
                run(transpose_a, step + TRANSPOSE_AHEAD - 1, TILES)
                run(transpose_a, step + TRANSPOSE_AHEAD, TILES)
                if step > 1:
                    run(transpose_h1, (step + 1) // PAIR, CHUNKS)
            if step == -1:
                spread_rows()
            if step - 4 in SCALAR_TILES:
                turn_back(step - 4)
            if step - 3 not in SCALAR_TILES:
                run(finish, step - 3, TILES)
